import numpy as np
import ml_dtypes


def mxq(x, axis, fmt="e4m3"):
    dtype, down = {"e4m3": (ml_dtypes.float8_e4m3fn, 7), "e5m2": (ml_dtypes.float8_e5m2, 14)}[fmt]
    v = np.moveaxis(np.asarray(x, np.float32).astype(ml_dtypes.bfloat16).astype(np.float64), axis, -1)
    blocks = v.reshape(v.shape[:-1] + (-1, 32))
    amax = np.abs(blocks).max(-1, keepdims=True)
    byte = np.maximum(np.where(amax > 0, np.frexp(amax)[1] - 1 + 127, 0) - down, 1)
    scale = np.exp2(byte - 127.0)
    codes = (blocks / scale).astype(np.float32).astype(dtype).astype(np.float64)
    return np.moveaxis((codes * scale).reshape(v.shape), -1, axis)


WIDE = False


def mx_kscale(k):
    if not WIDE:
        return np.ones(k)
    levels = np.array([10, -10, 5, -5, 0])
    a = np.random.permutation(np.resize(levels, k // 512 * 4)).reshape(k // 512, 4)
    idx = np.arange(k)
    return np.exp2(a[idx // 512, idx % 128 // 32])


BF16 = ml_dtypes.bfloat16


def bf(x):
    return np.asarray(x, np.float32).astype(BF16)


def f64(x):
    return np.asarray(x).astype(np.float64)


B, C_IN, C_OUT, H, W = 2, 8192, 64, 16, 32
P = 4
G = P * P


def setup_inputs():
    s = mx_kscale(C_IN)
    bound = np.sqrt(6.0 / (C_IN + C_OUT))
    return {"x": bf(np.random.standard_normal((B, C_IN, H, W)) * s[None, :, None, None]),
            "Wg": bf(np.random.uniform(-bound, bound, (G, C_OUT, C_IN)) / s[None, None, :]),
            "bg": bf(np.random.standard_normal((G, C_OUT)) * 0.25)}


def reference(x, Wg, bg):
    Bb, C, Hh, Ww = x.shape
    H4, W4 = Hh // P, Ww // P
    xq = mxq(f64(x), 1, "e4m3")
    wq = mxq(f64(Wg), 2, "e4m3")
    xg = xq.reshape(Bb, C, H4, P, W4, P).transpose(0, 2, 4, 3, 5, 1)
    xg = xg.reshape(Bb * H4 * W4, G, C).transpose(1, 0, 2)
    y = xg @ wq.transpose(0, 2, 1)
    O = y.shape[-1]
    y = y.transpose(1, 0, 2).reshape(Bb, H4, W4, G, O) + f64(bg)
    y = y.reshape(Bb, H4, W4, P, P, O).transpose(0, 5, 1, 3, 2, 4)
    return y.reshape(Bb, O, Hh, Ww)

@@ -1,0 +1,185 @@
+import concourse.mybir as mybir
+from concourse.masks import make_identity
+
+FLOPS = 2 * 16 * 64 * 64 * 8192
+
+F32 = mybir.dt.float32
+BF16 = mybir.dt.bfloat16
+U32 = mybir.dt.uint32
+U8 = mybir.dt.uint8
+FP8X4 = mybir.dt.float8_e4m3fn_x4
+ADD = mybir.AluOpType.add
+
+P = 128
+PACK = 4
+K_PASS = P * PACK
+
+BATCH, CHANNELS, OUT_CH, ROWS, COLS = 2, 8192, 64, 16, 32
+GRID = 4
+PIXELS = ROWS * COLS
+QUADS = PIXELS // GRID
+PASSES = CHANNELS // K_PASS
+CHUNK = 4
+CHUNKS = PASSES // CHUNK
+UNITS = 4
+N_MOVING = BATCH * QUADS
+
+VECTOR_QUADS = 80
+
+
+def tile_groupwiselinearprojector_k_kernel(tc, x, Wg, bg, out):
+    nc = tc.nc
+    w_rows = Wg.rearrange("g o k -> (g o) k").rearrange("(h a p) k -> a p h k", h=2, a=UNITS)
+
+    with (
+        tc.tile_pool(name="consts", bufs=1) as consts,
+        tc.tile_pool(name="raw", bufs=6) as raw,
+        tc.tile_pool(name="grouped", bufs=3) as grouped,
+        tc.tile_pool(name="x_ops", bufs=2 * CHUNK + 2) as x_ops,
+        tc.tile_pool(name="w_ops", bufs=3) as w_ops,
+        tc.psum_pool(name="psum_t", bufs=4) as psum_t,
+        tc.psum_pool(name="psum_acc", bufs=4) as psum_acc,
+    ):
+        ident = consts.tile([P, P], F32)
+        make_identity(nc, ident[:])
+
+        bg_sb = consts.tile([8, P], BF16)
+        nc.scalar.dma_start(
+            out=bg_sb[:].rearrange("s (h o) -> s h o", h=2),
+            in_=bg.rearrange("(h s) o -> s h o", h=2),
+        )
+        bias_rows = consts.tile([P, P], F32)
+        nc.vector.memset(bias_rows[:], 0.0)
+        nc.vector.tensor_copy(out=bias_rows[0:8, :], in_=bg_sb[:])
+        bias_ps = psum_t.tile([P, 4 * P], F32, tag="wt")
+        nc.tensor.transpose(bias_ps[:, 0:P], bias_rows[:], ident[:])
+        bias_sb = consts.tile([P, 8], F32)
+        nc.vector.tensor_copy(out=bias_sb[:], in_=bias_ps[:, 0:8])
+
+        sums = consts.tile([P, 2, GRID, 8, 2, 8], F32)
+        out_sb = consts.tile([P, BATCH * PIXELS // 2], F32)
+
+        raw_x, grouped_x, x_operand = {}, {}, {}
+        raw_w, grouped_w, w_operand, acc = {}, {}, {}, {}
+
+        def load_x(c):
+            raw_x[c] = raw.tile([P, BATCH, PACK, PIXELS], BF16, name="raw_x")
+            for b in range(BATCH):
+                nc.sync.dma_start(
+                    out=raw_x[c][:, b].rearrange("p (u e) x -> p u (e x)", u=2),
+                    in_=x[b, c * K_PASS : (c + 1) * K_PASS].rearrange("(u p e) r w -> p u (e r w)", u=2, e=2),
+                )
+
+        def regroup_x(c):
+            grouped_x[c] = grouped.tile([P, GRID, N_MOVING, PACK], BF16, align_bytes=64, name="grouped_x")
+            for b in range(BATCH):
+                src = raw_x[c][:, b].rearrange("p t (m i) -> p m t i", i=GRID)
+                dst = grouped_x[c][:, :, b * QUADS : (b + 1) * QUADS, :].rearrange("p i m t -> p m t i")
+                nc.vector.tensor_copy(out=dst[:, 0:VECTOR_QUADS], in_=src[:, 0:VECTOR_QUADS])
+                nc.scalar.copy(out=dst[:, VECTOR_QUADS:QUADS], in_=src[:, VECTOR_QUADS:QUADS])
+
+        def quantise_x(c):
+            x_codes = x_ops.tile([P, GRID * N_MOVING], U32, align_bytes=64)
+            x_scales = x_ops.tile([P, GRID * N_MOVING], U8, align_bytes=64)
+            nc.vector.quantize_mx(
+                out=x_codes[:].bitcast(FP8X4),
+                scales=x_scales[:],
+                in_=grouped_x[c][:].rearrange("p i m t -> p (i m t)"),
+            )
+            x_operand[c] = (x_codes, x_scales)
+
+        def load_w(j):
+            n, a = divmod(j, UNITS)
+            raw_w[j] = raw.tile([P, 2 * CHUNK * K_PASS], BF16, name="raw_w")
+            nc.sync.dma_start(
+                out=raw_w[j][:].rearrange("p (h k) -> p h k", h=2),
+                in_=w_rows[a][:, :, n * CHUNK * K_PASS : (n + 1) * CHUNK * K_PASS],
+            )
+
+        def transpose_w(j):
+            raw_words = raw_w[j][:].bitcast(F32).rearrange("p (h c u q) -> p h c u q", h=2, c=CHUNK, u=2)
+            grouped_w[j] = grouped.tile([P, CHUNK * 2 * P * PACK], BF16, align_bytes=64, name="grouped_w")
+            grouped_words = grouped_w[j][:].bitcast(F32).rearrange(
+                "p (c g h o u) -> p c g h o u", c=CHUNK, g=2, h=2, o=OUT_CH
+            )
+            for c in range(CHUNK):
+                wt = psum_t.tile([P, 2, 2, P], F32, tag="wt")
+                for h in range(2):
+                    for u in range(2):
+                        nc.tensor.transpose(wt[:, h, u, :], raw_words[:, h, c, u, :], ident[:])
+                for h in range(2):
+                    nc.scalar.copy(
+                        out=grouped_words[:, c, :, h, :, :],
+                        in_=wt[:, h].rearrange("p u (g o) -> p g o u", g=2),
+                    )
+
+        def quantise_w(j):
+            w_codes = w_ops.tile([P, CHUNK * 2 * P], U32, align_bytes=64)
+            w_scales = w_ops.tile([P, CHUNK * 2 * P], U8, align_bytes=64)
+            nc.vector.quantize_mx(out=w_codes[:].bitcast(FP8X4), scales=w_scales[:], in_=grouped_w[j][:])
+            w_operand[j] = (w_codes, w_scales)
+
+        def multiply(j):
+            n, a = divmod(j, UNITS)
+            w_codes, w_scales = w_operand[j]
+            acc[j] = psum_acc.tile([P, 2, N_MOVING], F32, name="acc")
+            for g in range(2):
+                i = 2 * (a % 2) + g
+                for c in range(CHUNK):
+                    x_codes, x_scales = x_operand[n * CHUNK + c]
+                    m_cols = slice((c * 2 + g) * P, (c * 2 + g + 1) * P)
+                    n_cols = slice(i * N_MOVING, (i + 1) * N_MOVING)
+                    nc.tensor.matmul_mx(
+                        out=acc[j][:, g, :],
+                        lhsT=w_codes[:, m_cols].bitcast(FP8X4),
+                        lhsT_scale=w_scales[:, m_cols],
+                        rhs=x_codes[:, n_cols].bitcast(FP8X4),
+                        rhs_scale=x_scales[:, n_cols],
+                        start=(c == 0),
+                        stop=(c == CHUNK - 1),
+                    )
+
+        def add_up(j):
+            n, a = divmod(j, UNITS)
+            l = a // 2
+            fresh = acc[j][:].rearrange("p g (m l w) -> p g m l w", l=2, w=8)[:, :, :, l, :]
+            total = sums[:, l, 2 * (a % 2) : 2 * (a % 2) + 2].rearrange("p g n z w -> p g (n z) w")
+            if n == 0:
+                before = bias_sb[:, 2 * a : 2 * a + 2].unsqueeze(2).unsqueeze(3).to_broadcast([P, 2, 16, 8])
+            else:
+                before = total
+            nc.vector.tensor_tensor(out=total, in0=fresh, in1=before, op=ADD)
+
+        with tc.manual_schedule():
+            for step in range(PASSES + CHUNK + 2):
+                j = step - CHUNK
+                if step < PASSES:
+                    load_x(step)
+                if 0 <= j < PASSES:
+                    load_w(j)
+                if step < PASSES:
+                    regroup_x(step)
+                if 0 <= j < PASSES:
+                    transpose_w(j)
+                if 0 <= j - 1 < PASSES:
+                    quantise_w(j - 1)
+                    multiply(j - 1)
+                if 0 <= step - 1 < PASSES:
+                    quantise_x(step - 1)
+                if 0 <= j - 2 < PASSES:
+                    add_up(j - 2)
+
+        for z in range(2):
+            rows = slice(z * OUT_CH, (z + 1) * OUT_CH)
+            copy = nc.vector.tensor_copy if z == 0 else nc.scalar.copy
+            for l in range(2):
+                copy(
+                    out=out_sb[rows, :].rearrange("p (n l w i) -> p l n w i", l=2, w=8, i=GRID)[:, l],
+                    in_=sums[rows, l, :, :, z, :].rearrange("p i n w -> p n w i"),
+                )
+            for b in range(BATCH):
+                queue = nc.sync if b == 0 else nc.scalar
+                queue.dma_start(
+                    out=out[b].rearrange("o (n z l) c -> z o n (l c)", z=2, l=2)[z],
+                    in_=out_sb[rows, b * 256 : (b + 1) * 256].rearrange("p (n x) -> p n x", n=4),
+                )

@@ -24,7 +24,7 @@ CHUNKS = PASSES // CHUNK
 UNITS = 4
 N_MOVING = BATCH * QUADS
 
-VECTOR_QUADS = 80
+VECTOR_QUADS = 96
 
 
 def tile_groupwiselinearprojector_k_kernel(tc, x, Wg, bg, out):

@@ -22,9 +22,10 @@ PASSES = CHANNELS // K_PASS
 CHUNK = 4
 CHUNKS = PASSES // CHUNK
 UNITS = 4
+N_UNITS = CHUNKS * UNITS
 N_MOVING = BATCH * QUADS
 
-VECTOR_QUADS = 96
+VECTOR_QUADS = 80
 
 
 def tile_groupwiselinearprojector_k_kernel(tc, x, Wg, bg, out):
@@ -36,7 +37,7 @@ def tile_groupwiselinearprojector_k_kernel(tc, x, Wg, bg, out):
         tc.tile_pool(name="raw", bufs=6) as raw,
         tc.tile_pool(name="grouped", bufs=3) as grouped,
         tc.tile_pool(name="x_ops", bufs=2 * CHUNK + 2) as x_ops,
-        tc.tile_pool(name="w_ops", bufs=3) as w_ops,
+        tc.tile_pool(name="w_ops", bufs=5) as w_ops,
         tc.psum_pool(name="psum_t", bufs=4) as psum_t,
         tc.psum_pool(name="psum_acc", bufs=4) as psum_acc,
     ):
@@ -60,7 +61,11 @@ def tile_groupwiselinearprojector_k_kernel(tc, x, Wg, bg, out):
         out_sb = consts.tile([P, BATCH * PIXELS // 2], F32)
 
         raw_x, grouped_x, x_operand = {}, {}, {}
-        raw_w, grouped_w, w_operand, acc = {}, {}, {}, {}
+        raw_w, grouped_w = {}, {}
+        w_operand = {}
+        acc = {}
+
+        pieces = [(j, 0, CHUNK) for j in range(N_UNITS - 1)] + [(N_UNITS - 1, c, 1) for c in range(CHUNK)]
 
         def load_x(c):
             raw_x[c] = raw.tile([P, BATCH, PACK, PIXELS], BF16, name="raw_x")
@@ -88,21 +93,24 @@ def tile_groupwiselinearprojector_k_kernel(tc, x, Wg, bg, out):
             )
             x_operand[c] = (x_codes, x_scales)
 
-        def load_w(j):
+        def load_w(q):
+            j, first, passes = pieces[q]
             n, a = divmod(j, UNITS)
-            raw_w[j] = raw.tile([P, 2 * CHUNK * K_PASS], BF16, name="raw_w")
+            k0 = (n * CHUNK + first) * K_PASS
+            raw_w[q] = raw.tile([P, 2 * passes * K_PASS], BF16, name="raw_w")
             nc.sync.dma_start(
-                out=raw_w[j][:].rearrange("p (h k) -> p h k", h=2),
-                in_=w_rows[a][:, :, n * CHUNK * K_PASS : (n + 1) * CHUNK * K_PASS],
+                out=raw_w[q][:].rearrange("p (h k) -> p h k", h=2),
+                in_=w_rows[a][:, :, k0 : k0 + passes * K_PASS],
             )
 
-        def transpose_w(j):
-            raw_words = raw_w[j][:].bitcast(F32).rearrange("p (h c u q) -> p h c u q", h=2, c=CHUNK, u=2)
-            grouped_w[j] = grouped.tile([P, CHUNK * 2 * P * PACK], BF16, align_bytes=64, name="grouped_w")
-            grouped_words = grouped_w[j][:].bitcast(F32).rearrange(
-                "p (c g h o u) -> p c g h o u", c=CHUNK, g=2, h=2, o=OUT_CH
+        def transpose_w(q):
+            j, first, passes = pieces[q]
+            raw_words = raw_w[q][:].bitcast(F32).rearrange("p (h c u q) -> p h c u q", h=2, c=passes, u=2)
+            grouped_w[q] = grouped.tile([P, passes * 2 * P * PACK], BF16, align_bytes=64, name="grouped_w")
+            grouped_words = grouped_w[q][:].bitcast(F32).rearrange(
+                "p (c g h o u) -> p c g h o u", c=passes, g=2, h=2, o=OUT_CH
             )
-            for c in range(CHUNK):
+            for c in range(passes):
                 wt = psum_t.tile([P, 2, 2, P], F32, tag="wt")
                 for h in range(2):
                     for u in range(2):
@@ -113,21 +121,29 @@ def tile_groupwiselinearprojector_k_kernel(tc, x, Wg, bg, out):
                         in_=wt[:, h].rearrange("p u (g o) -> p g o u", g=2),
                     )
 
-        def quantise_w(j):
-            w_codes = w_ops.tile([P, CHUNK * 2 * P], U32, align_bytes=64)
-            w_scales = w_ops.tile([P, CHUNK * 2 * P], U8, align_bytes=64)
-            nc.vector.quantize_mx(out=w_codes[:].bitcast(FP8X4), scales=w_scales[:], in_=grouped_w[j][:])
-            w_operand[j] = (w_codes, w_scales)
+        def quantise_w(q):
+            j, first, passes = pieces[q]
+            w_codes = w_ops.tile([P, passes * 2 * P], U32, align_bytes=64)
+            w_scales = w_ops.tile([P, passes * 2 * P], U8, align_bytes=64)
+            nc.vector.quantize_mx(out=w_codes[:].bitcast(FP8X4), scales=w_scales[:], in_=grouped_w[q][:])
+            for c in range(passes):
+                w_operand[(j, first + c)] = (w_codes[:, c * 2 * P : (c + 1) * 2 * P], w_scales[:, c * 2 * P : (c + 1) * 2 * P])
+
+        def unit_completed_by(q):
+            if not 0 <= q < len(pieces):
+                return None
+            j, first, passes = pieces[q]
+            return j if first + passes == CHUNK else None
 
         def multiply(j):
             n, a = divmod(j, UNITS)
-            w_codes, w_scales = w_operand[j]
             acc[j] = psum_acc.tile([P, 2, N_MOVING], F32, name="acc")
             for g in range(2):
                 i = 2 * (a % 2) + g
                 for c in range(CHUNK):
                     x_codes, x_scales = x_operand[n * CHUNK + c]
-                    m_cols = slice((c * 2 + g) * P, (c * 2 + g + 1) * P)
+                    w_codes, w_scales = w_operand[(j, c)]
+                    m_cols = slice(g * P, (g + 1) * P)
                     n_cols = slice(i * N_MOVING, (i + 1) * N_MOVING)
                     nc.tensor.matmul_mx(
                         out=acc[j][:, g, :],
@@ -151,23 +167,24 @@ def tile_groupwiselinearprojector_k_kernel(tc, x, Wg, bg, out):
             nc.vector.tensor_tensor(out=total, in0=fresh, in1=before, op=ADD)
 
         with tc.manual_schedule():
-            for step in range(PASSES + CHUNK + 2):
-                j = step - CHUNK
+            for step in range(CHUNK + len(pieces) + 2):
+                q = step - CHUNK
                 if step < PASSES:
                     load_x(step)
-                if 0 <= j < PASSES:
-                    load_w(j)
+                if 0 <= q < len(pieces):
+                    load_w(q)
                 if step < PASSES:
                     regroup_x(step)
-                if 0 <= j < PASSES:
-                    transpose_w(j)
-                if 0 <= j - 1 < PASSES:
-                    quantise_w(j - 1)
-                    multiply(j - 1)
+                if 0 <= q < len(pieces):
+                    transpose_w(q)
+                if 0 <= q - 1 < len(pieces):
+                    quantise_w(q - 1)
+                if unit_completed_by(q - 1) is not None:
+                    multiply(unit_completed_by(q - 1))
                 if 0 <= step - 1 < PASSES:
                     quantise_x(step - 1)
-                if 0 <= j - 2 < PASSES:
-                    add_up(j - 2)
+                if unit_completed_by(q - 2) is not None:
+                    add_up(unit_completed_by(q - 2))
 
         for z in range(2):
             rows = slice(z * OUT_CH, (z + 1) * OUT_CH)

@@ -8,35 +8,26 @@ BF16 = mybir.dt.bfloat16
 U32 = mybir.dt.uint32
 U8 = mybir.dt.uint8
 FP8X4 = mybir.dt.float8_e4m3fn_x4
-ADD = mybir.AluOpType.add
 
 P = 128
 PACK = 4
 K_PASS = P * PACK
 
 BATCH, CHANNELS, OUT_CH, ROWS, COLS = 2, 8192, 64, 16, 32
-GRID = 4
 PIXELS = ROWS * COLS
-QUADS = PIXELS // GRID
 PASSES = CHANNELS // K_PASS
-CHUNK = 4
-CHUNKS = PASSES // CHUNK
-UNITS = 4
-N_UNITS = CHUNKS * UNITS
-N_MOVING = BATCH * QUADS
-
-VECTOR_QUADS = 80
+PIECE = 4
+OPERANDS = 8
 
 
 def tile_groupwiselinearprojector_k_kernel(tc, x, Wg, bg, out):
     nc = tc.nc
-    w_rows = Wg.rearrange("g o k -> (g o) k").rearrange("(h a p) k -> a p h k", h=2, a=UNITS)
+    w_rows = Wg.rearrange("g o k -> (g o) k").rearrange("(l z e p) k -> l e p z k", l=2, z=2, e=2)
 
     with (
         tc.tile_pool(name="consts", bufs=1) as consts,
         tc.tile_pool(name="raw", bufs=6) as raw,
-        tc.tile_pool(name="grouped", bufs=3) as grouped,
-        tc.tile_pool(name="x_ops", bufs=2 * CHUNK + 2) as x_ops,
+        tc.tile_pool(name="grouped", bufs=4) as grouped,
         tc.tile_pool(name="w_ops", bufs=5) as w_ops,
         tc.psum_pool(name="psum_t", bufs=4) as psum_t,
         tc.psum_pool(name="psum_acc", bufs=4) as psum_acc,
@@ -44,31 +35,35 @@ def tile_groupwiselinearprojector_k_kernel(tc, x, Wg, bg, out):
         ident = consts.tile([P, P], F32)
         make_identity(nc, ident[:])
 
-        bg_sb = consts.tile([8, P], BF16)
-        nc.scalar.dma_start(
-            out=bg_sb[:].rearrange("s (h o) -> s h o", h=2),
-            in_=bg.rearrange("(h s) o -> s h o", h=2),
-        )
+        bg_sb = consts.tile([OPERANDS, P], BF16)
+        for l in range(2):
+            nc.scalar.dma_start(
+                out=bg_sb[4 * l : 4 * l + 4, :].rearrange("i (z o) -> i z o", z=2),
+                in_=bg.rearrange("(l z i) o -> l i z o", l=2, z=2)[l],
+            )
         bias_rows = consts.tile([P, P], F32)
         nc.vector.memset(bias_rows[:], 0.0)
-        nc.vector.tensor_copy(out=bias_rows[0:8, :], in_=bg_sb[:])
+        nc.vector.tensor_copy(out=bias_rows[0:OPERANDS, :], in_=bg_sb[:])
         bias_ps = psum_t.tile([P, 4 * P], F32, tag="wt")
         nc.tensor.transpose(bias_ps[:, 0:P], bias_rows[:], ident[:])
-        bias_sb = consts.tile([P, 8], F32)
-        nc.vector.tensor_copy(out=bias_sb[:], in_=bias_ps[:, 0:8])
+        bias_sb = consts.tile([P, OPERANDS], F32)
+        nc.vector.tensor_copy(out=bias_sb[:], in_=bias_ps[:, 0:OPERANDS])
 
-        sums = consts.tile([P, 2, GRID, 8, 2, 8], F32)
+        x_codes = consts.tile([P, PASSES, OPERANDS * P], U32, align_bytes=64)
+        x_scales = consts.tile([P, PASSES, OPERANDS * P], U8, align_bytes=64)
+        result = consts.tile([P, 2, 4, 8, 2, 8], F32)
         out_sb = consts.tile([P, BATCH * PIXELS // 2], F32)
 
-        raw_x, grouped_x, x_operand = {}, {}, {}
+        raw_x, grouped_x = {}, {}
         raw_w, grouped_w = {}, {}
         w_operand = {}
         acc = {}
 
-        pieces = [(j, 0, CHUNK) for j in range(N_UNITS - 1)] + [(N_UNITS - 1, c, 1) for c in range(CHUNK)]
+        pieces = [(a, first, PIECE) for a in range(4) for first in range(0, PASSES, PIECE)]
+        pieces = pieces[:-1] + [(3, first, 1) for first in range(PASSES - PIECE, PASSES)]
 
         def load_x(c):
-            raw_x[c] = raw.tile([P, BATCH, PACK, PIXELS], BF16, name="raw_x")
+            raw_x[c] = raw.tile([P, BATCH, PACK, PIXELS], BF16, name="raw_x", tag="raw")
             for b in range(BATCH):
                 nc.sync.dma_start(
                     out=raw_x[c][:, b].rearrange("p (u e) x -> p u (e x)", u=2),
@@ -76,127 +71,120 @@ def tile_groupwiselinearprojector_k_kernel(tc, x, Wg, bg, out):
                 )
 
         def regroup_x(c):
-            grouped_x[c] = grouped.tile([P, GRID, N_MOVING, PACK], BF16, align_bytes=64, name="grouped_x")
-            for b in range(BATCH):
-                src = raw_x[c][:, b].rearrange("p t (m i) -> p m t i", i=GRID)
-                dst = grouped_x[c][:, :, b * QUADS : (b + 1) * QUADS, :].rearrange("p i m t -> p m t i")
-                nc.vector.tensor_copy(out=dst[:, 0:VECTOR_QUADS], in_=src[:, 0:VECTOR_QUADS])
-                nc.scalar.copy(out=dst[:, VECTOR_QUADS:QUADS], in_=src[:, VECTOR_QUADS:QUADS])
+            grouped_x[c] = grouped.tile([P, 2, 4, P, PACK], BF16, align_bytes=64, name="grouped_x", tag="grouped")
+            src = raw_x[c][:].rearrange("p b t (h l m i) -> p b l h m t i", h=4, l=2, i=4)
+            dst = grouped_x[c][:].rearrange("p l i (b h m) t -> p b l h m t i", b=BATCH, h=4)
+            for l in range(2):
+                nc.vector.tensor_copy(out=dst[:, 0, l], in_=src[:, 0, l])
+                for h in range(4):
+                    nc.scalar.copy(out=dst[:, 1, l, h], in_=src[:, 1, l, h])
 
         def quantise_x(c):
-            x_codes = x_ops.tile([P, GRID * N_MOVING], U32, align_bytes=64)
-            x_scales = x_ops.tile([P, GRID * N_MOVING], U8, align_bytes=64)
             nc.vector.quantize_mx(
-                out=x_codes[:].bitcast(FP8X4),
-                scales=x_scales[:],
-                in_=grouped_x[c][:].rearrange("p i m t -> p (i m t)"),
+                out=x_codes[:, c, :].bitcast(FP8X4),
+                scales=x_scales[:, c, :],
+                in_=grouped_x[c][:].rearrange("p l i m t -> p (l i m t)"),
             )
-            x_operand[c] = (x_codes, x_scales)
 
         def load_w(q):
-            j, first, passes = pieces[q]
-            n, a = divmod(j, UNITS)
-            k0 = (n * CHUNK + first) * K_PASS
-            raw_w[q] = raw.tile([P, 2 * passes * K_PASS], BF16, name="raw_w")
+            a, first, passes = pieces[q]
+            raw_w[q] = raw.tile([P, 2 * passes * K_PASS], BF16, name="raw_w", tag="raw")
             nc.sync.dma_start(
-                out=raw_w[q][:].rearrange("p (h k) -> p h k", h=2),
-                in_=w_rows[a][:, :, k0 : k0 + passes * K_PASS],
+                out=raw_w[q][:].rearrange("p (z k) -> p z k", z=2),
+                in_=w_rows[a // 2, a % 2][:, :, first * K_PASS : (first + passes) * K_PASS],
             )
 
         def transpose_w(q):
-            j, first, passes = pieces[q]
-            raw_words = raw_w[q][:].bitcast(F32).rearrange("p (h c u q) -> p h c u q", h=2, c=passes, u=2)
-            grouped_w[q] = grouped.tile([P, passes * 2 * P * PACK], BF16, align_bytes=64, name="grouped_w")
+            a, first, passes = pieces[q]
+            raw_words = raw_w[q][:].bitcast(F32).rearrange("p (z c u q) -> p z c u q", z=2, c=passes, u=2)
+            grouped_w[q] = grouped.tile([P, passes * 2 * P * PACK], BF16, align_bytes=64, name="grouped_w", tag="grouped")
             grouped_words = grouped_w[q][:].bitcast(F32).rearrange(
-                "p (c g h o u) -> p c g h o u", c=passes, g=2, h=2, o=OUT_CH
+                "p (c g z o u) -> p c g z o u", c=passes, g=2, z=2, o=OUT_CH
             )
             for c in range(passes):
                 wt = psum_t.tile([P, 2, 2, P], F32, tag="wt")
-                for h in range(2):
+                for z in range(2):
                     for u in range(2):
-                        nc.tensor.transpose(wt[:, h, u, :], raw_words[:, h, c, u, :], ident[:])
-                for h in range(2):
-                    nc.scalar.copy(
-                        out=grouped_words[:, c, :, h, :, :],
-                        in_=wt[:, h].rearrange("p u (g o) -> p g o u", g=2),
+                        nc.tensor.transpose(wt[:, z, u, :], raw_words[:, z, c, u, :], ident[:])
+                copy = nc.vector.tensor_copy if (first + c) % 4 == 3 else nc.scalar.copy
+                for z in range(2):
+                    copy(
+                        out=grouped_words[:, c, :, z, :, :],
+                        in_=wt[:, z].rearrange("p u (g o) -> p g o u", g=2),
                     )
 
         def quantise_w(q):
-            j, first, passes = pieces[q]
+            a, first, passes = pieces[q]
             w_codes = w_ops.tile([P, passes * 2 * P], U32, align_bytes=64)
             w_scales = w_ops.tile([P, passes * 2 * P], U8, align_bytes=64)
             nc.vector.quantize_mx(out=w_codes[:].bitcast(FP8X4), scales=w_scales[:], in_=grouped_w[q][:])
             for c in range(passes):
-                w_operand[(j, first + c)] = (w_codes[:, c * 2 * P : (c + 1) * 2 * P], w_scales[:, c * 2 * P : (c + 1) * 2 * P])
+                cols = slice(c * 2 * P, (c + 1) * 2 * P)
+                w_operand[(a, first + c)] = (w_codes[:, cols], w_scales[:, cols])
 
-        def unit_completed_by(q):
-            if not 0 <= q < len(pieces):
-                return None
-            j, first, passes = pieces[q]
-            return j if first + passes == CHUNK else None
-
-        def multiply(j):
-            n, a = divmod(j, UNITS)
-            acc[j] = psum_acc.tile([P, 2, N_MOVING], F32, name="acc")
+        def multiply(q):
+            a, first, passes = pieces[q]
             for g in range(2):
-                i = 2 * (a % 2) + g
-                for c in range(CHUNK):
-                    x_codes, x_scales = x_operand[n * CHUNK + c]
-                    w_codes, w_scales = w_operand[(j, c)]
+                if first == 0:
+                    acc[(a, g)] = psum_acc.tile([P, P], F32, name="acc")
+                pair = 4 * (a // 2) + 2 * (a % 2) + g
+                for c in range(first, first + passes):
+                    w_codes, w_scales = w_operand[(a, c)]
                     m_cols = slice(g * P, (g + 1) * P)
-                    n_cols = slice(i * N_MOVING, (i + 1) * N_MOVING)
+                    n_cols = slice(pair * P, (pair + 1) * P)
                     nc.tensor.matmul_mx(
-                        out=acc[j][:, g, :],
+                        out=acc[(a, g)][:],
                         lhsT=w_codes[:, m_cols].bitcast(FP8X4),
                         lhsT_scale=w_scales[:, m_cols],
-                        rhs=x_codes[:, n_cols].bitcast(FP8X4),
-                        rhs_scale=x_scales[:, n_cols],
+                        rhs=x_codes[:, c, n_cols].bitcast(FP8X4),
+                        rhs_scale=x_scales[:, c, n_cols],
                         start=(c == 0),
-                        stop=(c == CHUNK - 1),
+                        stop=(c == PASSES - 1),
                     )
 
-        def add_up(j):
-            n, a = divmod(j, UNITS)
-            l = a // 2
-            fresh = acc[j][:].rearrange("p g (m l w) -> p g m l w", l=2, w=8)[:, :, :, l, :]
-            total = sums[:, l, 2 * (a % 2) : 2 * (a % 2) + 2].rearrange("p g n z w -> p g (n z) w")
-            if n == 0:
-                before = bias_sb[:, 2 * a : 2 * a + 2].unsqueeze(2).unsqueeze(3).to_broadcast([P, 2, 16, 8])
-            else:
-                before = total
-            nc.vector.tensor_tensor(out=total, in0=fresh, in1=before, op=ADD)
+        def add_bias(q):
+            if not 0 <= q < len(pieces):
+                return
+            a, first, passes = pieces[q]
+            if first + passes < PASSES:
+                return
+            for g in range(2):
+                l, i = a // 2, 2 * (a % 2) + g
+                nc.vector.tensor_scalar_add(
+                    out=result[:, l, i].rearrange("p n z w -> p (n z w)"),
+                    in0=acc[(a, g)][:],
+                    scalar1=bias_sb[:, 4 * l + i : 4 * l + i + 1],
+                )
 
         with tc.manual_schedule():
-            for step in range(CHUNK + len(pieces) + 2):
-                q = step - CHUNK
-                if step < PASSES:
-                    load_x(step)
-                if 0 <= q < len(pieces):
+            for c in range(PASSES + 1):
+                if c < PASSES:
+                    load_x(c)
+                    regroup_x(c)
+                if c >= 1:
+                    quantise_x(c - 1)
+            for q in range(len(pieces) + 2):
+                if q < len(pieces):
                     load_w(q)
-                if step < PASSES:
-                    regroup_x(step)
-                if 0 <= q < len(pieces):
-                    transpose_w(q)
                 if 0 <= q - 1 < len(pieces):
                     quantise_w(q - 1)
-                if unit_completed_by(q - 1) is not None:
-                    multiply(unit_completed_by(q - 1))
-                if 0 <= step - 1 < PASSES:
-                    quantise_x(step - 1)
-                if unit_completed_by(q - 2) is not None:
-                    add_up(unit_completed_by(q - 2))
+                if q < len(pieces):
+                    transpose_w(q)
+                if 0 <= q - 1 < len(pieces):
+                    multiply(q - 1)
+                add_bias(q - 2)
 
         for z in range(2):
             rows = slice(z * OUT_CH, (z + 1) * OUT_CH)
             copy = nc.vector.tensor_copy if z == 0 else nc.scalar.copy
             for l in range(2):
                 copy(
-                    out=out_sb[rows, :].rearrange("p (n l w i) -> p l n w i", l=2, w=8, i=GRID)[:, l],
-                    in_=sums[rows, l, :, :, z, :].rearrange("p i n w -> p n w i"),
+                    out=out_sb[rows, :].rearrange("p (n l w i) -> p l n w i", l=2, w=8, i=4)[:, l],
+                    in_=result[rows, l, :, :, z, :].rearrange("p i n w -> p n w i"),
                 )
             for b in range(BATCH):
                 queue = nc.sync if b == 0 else nc.scalar
                 queue.dma_start(
-                    out=out[b].rearrange("o (n z l) c -> z o n (l c)", z=2, l=2)[z],
-                    in_=out_sb[rows, b * 256 : (b + 1) * 256].rearrange("p (n x) -> p n x", n=4),
+                    out=out[b].rearrange("o (m z) c -> z o m c", z=2)[z],
+                    in_=out_sb[rows, b * 256 : (b + 1) * 256].rearrange("p (m c) -> p m c", c=COLS),
                 )

import concourse.mybir as mybir
from concourse.masks import make_identity

FLOPS = 2 * 16 * 64 * 64 * 8192

F32 = mybir.dt.float32
BF16 = mybir.dt.bfloat16
U32 = mybir.dt.uint32
U8 = mybir.dt.uint8
FP8X4 = mybir.dt.float8_e4m3fn_x4

P = 128
PACK = 4
K_PASS = P * PACK

BATCH, CHANNELS, OUT_CH, ROWS, COLS = 2, 8192, 64, 16, 32
PIXELS = ROWS * COLS
PASSES = CHANNELS // K_PASS
PIECE = 4
OPERANDS = 8


def tile_groupwiselinearprojector_k_kernel(tc, x, Wg, bg, out):
    nc = tc.nc
    w_rows = Wg.rearrange("g o k -> (g o) k").rearrange("(l z e p) k -> l e p z k", l=2, z=2, e=2)

    with (
        tc.tile_pool(name="consts", bufs=1) as consts,
        tc.tile_pool(name="raw", bufs=6) as raw,
        tc.tile_pool(name="grouped", bufs=4) as grouped,
        tc.tile_pool(name="w_ops", bufs=5) as w_ops,
        tc.psum_pool(name="psum_t", bufs=4) as psum_t,
        tc.psum_pool(name="psum_acc", bufs=4) as psum_acc,
    ):
        ident = consts.tile([P, P], F32)
        make_identity(nc, ident[:])

        bg_sb = consts.tile([OPERANDS, P], BF16)
        for l in range(2):
            nc.scalar.dma_start(
                out=bg_sb[4 * l : 4 * l + 4, :].rearrange("i (z o) -> i z o", z=2),
                in_=bg.rearrange("(l z i) o -> l i z o", l=2, z=2)[l],
            )
        bias_rows = consts.tile([P, P], F32)
        nc.vector.memset(bias_rows[:], 0.0)
        nc.vector.tensor_copy(out=bias_rows[0:OPERANDS, :], in_=bg_sb[:])
        bias_ps = psum_t.tile([P, 4 * P], F32, tag="wt")
        nc.tensor.transpose(bias_ps[:, 0:P], bias_rows[:], ident[:])
        bias_sb = consts.tile([P, OPERANDS], F32)
        nc.vector.tensor_copy(out=bias_sb[:], in_=bias_ps[:, 0:OPERANDS])

        x_codes = consts.tile([P, PASSES, OPERANDS * P], U32, align_bytes=64)
        x_scales = consts.tile([P, PASSES, OPERANDS * P], U8, align_bytes=64)
        result = consts.tile([P, 2, 4, 8, 2, 8], F32)
        out_sb = consts.tile([P, BATCH * PIXELS // 2], F32)

        raw_x, grouped_x = {}, {}
        raw_w, grouped_w = {}, {}
        w_operand = {}
        acc = {}

        pieces = [(a, first, PIECE) for a in range(4) for first in range(0, PASSES, PIECE)]
        pieces = pieces[:-1] + [(3, first, 1) for first in range(PASSES - PIECE, PASSES)]

        def load_x(c):
            raw_x[c] = raw.tile([P, BATCH, PACK, PIXELS], BF16, name="raw_x", tag="raw")
            for b in range(BATCH):
                nc.sync.dma_start(
                    out=raw_x[c][:, b].rearrange("p (u e) x -> p u (e x)", u=2),
                    in_=x[b, c * K_PASS : (c + 1) * K_PASS].rearrange("(u p e) r w -> p u (e r w)", u=2, e=2),
                )

        def regroup_x(c):
            grouped_x[c] = grouped.tile([P, 2, 4, P, PACK], BF16, align_bytes=64, name="grouped_x", tag="grouped")
            src = raw_x[c][:].rearrange("p b t (h l m i) -> p b l h m t i", h=4, l=2, i=4)
            dst = grouped_x[c][:].rearrange("p l i (b h m) t -> p b l h m t i", b=BATCH, h=4)
            for l in range(2):
                nc.vector.tensor_copy(out=dst[:, 0, l], in_=src[:, 0, l])
                for h in range(4):
                    nc.scalar.copy(out=dst[:, 1, l, h], in_=src[:, 1, l, h])

        def quantise_x(c):
            nc.vector.quantize_mx(
                out=x_codes[:, c, :].bitcast(FP8X4),
                scales=x_scales[:, c, :],
                in_=grouped_x[c][:].rearrange("p l i m t -> p (l i m t)"),
            )

        def load_w(q):
            a, first, passes = pieces[q]
            raw_w[q] = raw.tile([P, 2 * passes * K_PASS], BF16, name="raw_w", tag="raw")
            nc.sync.dma_start(
                out=raw_w[q][:].rearrange("p (z k) -> p z k", z=2),
                in_=w_rows[a // 2, a % 2][:, :, first * K_PASS : (first + passes) * K_PASS],
            )

        def transpose_w(q):
            a, first, passes = pieces[q]
            raw_words = raw_w[q][:].bitcast(F32).rearrange("p (z c u q) -> p z c u q", z=2, c=passes, u=2)
            grouped_w[q] = grouped.tile([P, passes * 2 * P * PACK], BF16, align_bytes=64, name="grouped_w", tag="grouped")
            grouped_words = grouped_w[q][:].bitcast(F32).rearrange(
                "p (c g z o u) -> p c g z o u", c=passes, g=2, z=2, o=OUT_CH
            )
            for c in range(passes):
                wt = psum_t.tile([P, 2, 2, P], F32, tag="wt")
                for z in range(2):
                    for u in range(2):
                        nc.tensor.transpose(wt[:, z, u, :], raw_words[:, z, c, u, :], ident[:])
                copy = nc.vector.tensor_copy if (first + c) % 4 == 3 else nc.scalar.copy
                for z in range(2):
                    copy(
                        out=grouped_words[:, c, :, z, :, :],
                        in_=wt[:, z].rearrange("p u (g o) -> p g o u", g=2),
                    )

        def quantise_w(q):
            a, first, passes = pieces[q]
            w_codes = w_ops.tile([P, passes * 2 * P], U32, align_bytes=64)
            w_scales = w_ops.tile([P, passes * 2 * P], U8, align_bytes=64)
            nc.vector.quantize_mx(out=w_codes[:].bitcast(FP8X4), scales=w_scales[:], in_=grouped_w[q][:])
            for c in range(passes):
                cols = slice(c * 2 * P, (c + 1) * 2 * P)
                w_operand[(a, first + c)] = (w_codes[:, cols], w_scales[:, cols])

        def multiply(q):
            a, first, passes = pieces[q]
            for g in range(2):
                if first == 0:
                    acc[(a, g)] = psum_acc.tile([P, P], F32, name="acc")
                pair = 4 * (a // 2) + 2 * (a % 2) + g
                for c in range(first, first + passes):
                    w_codes, w_scales = w_operand[(a, c)]
                    m_cols = slice(g * P, (g + 1) * P)
                    n_cols = slice(pair * P, (pair + 1) * P)
                    nc.tensor.matmul_mx(
                        out=acc[(a, g)][:],
                        lhsT=w_codes[:, m_cols].bitcast(FP8X4),
                        lhsT_scale=w_scales[:, m_cols],
                        rhs=x_codes[:, c, n_cols].bitcast(FP8X4),
                        rhs_scale=x_scales[:, c, n_cols],
                        start=(c == 0),
                        stop=(c == PASSES - 1),
                    )

        def add_bias(q):
            if not 0 <= q < len(pieces):
                return
            a, first, passes = pieces[q]
            if first + passes < PASSES:
                return
            for g in range(2):
                l, i = a // 2, 2 * (a % 2) + g
                nc.vector.tensor_scalar_add(
                    out=result[:, l, i].rearrange("p n z w -> p (n z w)"),
                    in0=acc[(a, g)][:],
                    scalar1=bias_sb[:, 4 * l + i : 4 * l + i + 1],
                )

        with tc.manual_schedule():
            for c in range(PASSES + 1):
                if c < PASSES:
                    load_x(c)
                    regroup_x(c)
                if c >= 1:
                    quantise_x(c - 1)
            for q in range(len(pieces) + 2):
                if q < len(pieces):
                    load_w(q)
                if 0 <= q - 1 < len(pieces):
                    quantise_w(q - 1)
                if q < len(pieces):
                    transpose_w(q)
                if 0 <= q - 1 < len(pieces):
                    multiply(q - 1)
                add_bias(q - 2)

        for z in range(2):
            rows = slice(z * OUT_CH, (z + 1) * OUT_CH)
            copy = nc.vector.tensor_copy if z == 0 else nc.scalar.copy
            for l in range(2):
                copy(
                    out=out_sb[rows, :].rearrange("p (n l w i) -> p l n w i", l=2, w=8, i=4)[:, l],
                    in_=result[rows, l, :, :, z, :].rearrange("p i n w -> p n w i"),
                )
            for b in range(BATCH):
                queue = nc.sync if b == 0 else nc.scalar
                queue.dma_start(
                    out=out[b].rearrange("o (m z) c -> z o m c", z=2)[z],
                    in_=out_sb[rows, b * 256 : (b + 1) * 256].rearrange("p (m c) -> p m c", c=COLS),
                )
